import numpy as np
import ml_dtypes


def mxq(x, axis, fmt="e4m3"):
    dtype, down = {"e4m3": (ml_dtypes.float8_e4m3fn, 7), "e5m2": (ml_dtypes.float8_e5m2, 14)}[fmt]
    v = np.moveaxis(np.asarray(x, np.float32).astype(ml_dtypes.bfloat16).astype(np.float64), axis, -1)
    blocks = v.reshape(v.shape[:-1] + (-1, 32))
    amax = np.abs(blocks).max(-1, keepdims=True)
    byte = np.maximum(np.where(amax > 0, np.frexp(amax)[1] - 1 + 127, 0) - down, 1)
    scale = np.exp2(byte - 127.0)
    codes = (blocks / scale).astype(np.float32).astype(dtype).astype(np.float64)
    return np.moveaxis((codes * scale).reshape(v.shape), -1, axis)


WIDE = False


def mx_kscale(k):
    if not WIDE:
        return np.ones(k)
    levels = np.array([30, -30])
    if k % 512:
        return np.exp2(np.random.permutation(np.resize(levels, k // 32))).repeat(32)
    a = np.empty((k // 512, 16))
    for p in range(k // 512):
        a[p, :8] = np.random.permutation(np.resize(levels, 8))
        for g in range(8):
            far = levels[np.abs(levels - a[p, g]) >= 10]
            a[p, g + 8] = far[np.random.randint(len(far))]
    return np.exp2(a.ravel()).repeat(32)


BF16 = ml_dtypes.bfloat16


def bf(x):
    return np.asarray(x, np.float32).astype(BF16)


def f64(x):
    return np.asarray(x).astype(np.float64)


E2M1 = np.array([0.0, 0.5, 1.0, 1.5, 2.0, 3.0, 4.0, 6.0, -0.0, -0.5, -1.0, -1.5, -2.0, -3.0, -4.0, -6.0])


def pack_weight(w, fmt):
    k, n = w.shape
    w = f64(bf(w)).reshape(k // 32, 32, n)
    amax = np.abs(w).max(1)
    if fmt == "e4m3":
        byte = np.frexp(amax)[1] - 1 + 127 - 7
    else:
        mant, ex = np.frexp(amax / 6.0)
        byte = np.where(mant > 0.5, ex, ex - 1) + 127
    byte = np.clip(np.where(amax > 0, byte, 1), 1, 254)
    scaled = (w * np.exp2(127.0 - byte)[:, None, :]).reshape(k, n).astype(np.float32)
    by_word = np.ascontiguousarray(scaled.reshape(k // 512, 128, 4, n).transpose(0, 1, 3, 2))
    if fmt == "e4m3":
        words = by_word.astype(ml_dtypes.float8_e4m3fn).view(np.uint8)
    else:
        c = by_word.astype(ml_dtypes.float4_e2m1fn).view(np.uint8) & 0xF
        words = c[..., 0::2] | (c[..., 1::2] << 4)
    return np.ascontiguousarray(words), np.ascontiguousarray(byte.astype(np.uint8).reshape(k // 512, 16, n))


def unpack_weight(words, scales, fmt):
    g, p, n, _ = words.shape
    if fmt == "e4m3":
        vals = np.ascontiguousarray(words).view(ml_dtypes.float8_e4m3fn).astype(np.float64)
    else:
        nib = np.empty((g, p, n, 4), np.uint8)
        nib[..., 0::2] = words & 0xF
        nib[..., 1::2] = words >> 4
        vals = E2M1[nib]
    vals = vals * np.repeat(np.exp2(scales.astype(np.float64) - 127.0), 8, axis=1)[..., None]
    return vals.transpose(0, 1, 3, 2).reshape(g * 512, n)

def pack4(w):
    words, scales = pack_weight(w, "e2m1")
    return words.reshape(words.shape[0], 128, -1), scales


def unpack4(words, scales):
    return unpack_weight(words.reshape(words.shape[0], 128, -1, 2), scales, "e2m1")


B, S, DIM, H, NOPE, ROPE, VHD, KV_RANK = 2, 256, 2048, 16, 128, 64, 128, 512
QKHD = NOPE + ROPE
HALF = ROPE // 2


def rope(u, cos, sin):
    ur = u.reshape(u.shape[:-1] + (HALF, 2))
    a, b = ur[..., 0], ur[..., 1]
    c = cos[None, :, None, :]
    s = sin[None, :, None, :]
    return np.stack([a * c - b * s, a * s + b * c], axis=-1).reshape(u.shape)


def setup_inputs():
    s = mx_kscale(DIM)
    inv_freq = 1.0 / 10000.0 ** (np.arange(0, ROPE, 2) / ROPE)
    ang = np.arange(S)[:, None] * inv_freq[None, :]
    x = bf(np.random.standard_normal((B, S, DIM)) * s)
    wq_w_words, wq_w_scales = pack4(np.random.standard_normal((DIM, H * QKHD)) / np.sqrt(DIM) / s[:, None])
    return {"x": x,
            "wq_w_words": wq_w_words, "wq_w_scales": wq_w_scales,
            "wq_b": bf(np.random.standard_normal(H * QKHD) * 0.2),
            "cos": bf(np.cos(ang)), "sin": bf(np.sin(ang))}


def reference(x, wq_w_words, wq_w_scales, wq_b, cos, sin):
    q = (mxq(f64(x), 2, "e5m2") @ unpack4(wq_w_words, wq_w_scales)) + f64(wq_b)
    q = q.reshape(B, S, H, QKHD)
    return np.concatenate([q[..., :NOPE], rope(q[..., NOPE:], f64(cos), f64(sin))], axis=-1)

@@ -1,0 +1,220 @@
+from contextlib import ExitStack
+
+import concourse.mybir as mybir
+from concourse.masks import make_identity
+
+B, S, DIM, H, NOPE, ROPE = 2, 256, 2048, 16, 128, 64
+TOKENS = B * S
+COLS = H * (NOPE + ROPE)
+FLOPS = 2 * TOKENS * DIM * COLS
+
+F32 = mybir.dt.float32
+BF16 = mybir.dt.bfloat16
+I32 = mybir.dt.int32
+U32 = mybir.dt.uint32
+U8 = mybir.dt.uint8
+E5M2X4 = mybir.dt.float8_e5m2_x4
+E2M1X4 = mybir.dt.float4_e2m1fn_x4
+ADD = mybir.AluOpType.add
+MULT = mybir.AluOpType.mult
+
+P = 128
+K_PASS = 512
+PASSES = DIM // K_PASS
+N_TILE = 512
+TOKEN_TILES = TOKENS // P
+COL_TILES = COLS // N_TILE
+HALF_K = DIM // 2
+BIAS_ROWS = 8
+BIAS_WIDTH = COLS // BIAS_ROWS
+CHUNK = ROPE
+CHUNKS = N_TILE // CHUNK
+WEIGHT_GROUPS = [(5, 6), (4, 5), (2, 4), (0, 2)]
+
+
+def tile_mla_pb_kernel(tc, x, wq_w_words, wq_w_scales, wq_b, cos, sin, out):
+    nc = tc.nc
+    x_rows = x.rearrange("b s k -> (b s) k")
+    out_rows = out.rearrange("b s h d -> (b s) (h d)")
+
+    with ExitStack() as ctx:
+        keep = ctx.enter_context(tc.tile_pool(name="keep", bufs=1))
+        stage = ctx.enter_context(tc.tile_pool(name="stage", bufs=3))
+        results = ctx.enter_context(tc.tile_pool(name="results", bufs=TOKEN_TILES * COL_TILES))
+        psum = ctx.enter_context(tc.psum_pool(name="psum", bufs=8))
+        ctx.enter_context(tc.manual_schedule())
+
+        ident = keep.tile([P, P], F32)
+        selector = keep.tile([P, BIAS_ROWS], BF16)
+        bias_rows = keep.tile([P, BIAS_WIDTH], BF16)
+        bias = keep.tile([P, COLS], BF16)
+        cos_sb = keep.tile([P, 2, ROPE // 2], BF16)
+        sin_sb = keep.tile([P, 2, ROPE // 2], BF16)
+        cos_pairs = keep.tile([P, 2, ROPE // 2, 2], F32)
+        sin_pairs = keep.tile([P, 2, ROPE // 2, 2], F32)
+        x_sb, codes, scales = {}, {}, {}
+        for half in range(2):
+            first_x = keep.tile([P, HALF_K], BF16, name="x_0_%d" % half)
+            x_sb[0, half] = first_x[:]
+        for tt in range(1, TOKEN_TILES):
+            whole_x = keep.tile([P, DIM], BF16, name="x_%d" % tt)
+            x_sb[tt] = whole_x[:]
+            for half in range(2):
+                x_sb[tt, half] = whole_x[:, half * HALF_K : (half + 1) * HALF_K]
+        for tt in range(TOKEN_TILES):
+            for half in range(2):
+                codes[tt, half] = keep.tile([P, 2 * P], U32, name="codes_%d_%d" % (tt, half), align_bytes=64)
+                scales[tt, half] = keep.tile([P, 2 * P], U8, name="scales_%d_%d" % (tt, half), align_bytes=64)
+        words, planes = {}, {}
+        for first, last in WEIGHT_GROUPS:
+            width = (last - first) * N_TILE
+            words[first] = keep.tile([P, PASSES, 2 * width], U8, name="words_%d" % first, align_bytes=64)
+            planes[first] = keep.tile([P, PASSES, width], U8, name="plane_%d" % first, align_bytes=64)
+
+        def load_x(tt):
+            nc.sync.dma_start(out=x_sb[tt], in_=x_rows[tt * P : (tt + 1) * P, :])
+
+        def load_weights(first, last):
+            plane = planes[first]
+            nc.vector.memset(plane[:].rearrange("p g n -> p (g n)").bitcast(I32), 0)
+            for r in range(4):
+                nc.sync.dma_start(
+                    out=plane[r:P:32, :, :].bitcast(I32),
+                    in_=wq_w_scales[:, r:16:4, first * N_TILE : last * N_TILE].rearrange("g q n -> q g n").bitcast(I32),
+                )
+            nc.sync.dma_start(
+                out=words[first][:].bitcast(I32),
+                in_=wq_w_words[:, :, 2 * first * N_TILE : 2 * last * N_TILE].rearrange("g p n -> p g n").bitcast(I32),
+            )
+
+        def spread_bias():
+            for pair in range(BIAS_ROWS // 2):
+                spread = psum.tile([P, 2 * BIAS_WIDTH], BF16, tag="bank")
+                for i in range(2):
+                    row = 2 * pair + i
+                    nc.tensor.matmul(
+                        out=spread[:, i * BIAS_WIDTH : (i + 1) * BIAS_WIDTH],
+                        lhsT=selector[:, row : row + 1].to_broadcast([P, P]),
+                        rhs=bias_rows[:],
+                        start=True,
+                        stop=True,
+                    )
+                nc.vector.tensor_copy(out=bias[:, 2 * pair * BIAS_WIDTH : 2 * (pair + 1) * BIAS_WIDTH], in_=spread[:])
+
+        def quantize_x(tt):
+            for half in range(2):
+                pairs = x_sb[tt, half].bitcast(F32)
+                turned = psum.tile([P, 2, 2, P], F32, tag="bank")
+                for g in range(2):
+                    for u in range(2):
+                        nc.tensor.transpose(turned[:, g, u, :], pairs[:, 256 * g + u : 256 * (g + 1) : 2], ident[:])
+                grouped = stage.tile([P, HALF_K], BF16, align_bytes=64)
+                nc.scalar.copy(
+                    out=grouped[:].bitcast(F32).rearrange("p (g r u) -> p g r u", g=2, u=2),
+                    in_=turned[:].rearrange("p g u r -> p g r u"),
+                )
+                nc.vector.quantize_mx(
+                    out=codes[tt, half][:].bitcast(E5M2X4), scales=scales[tt, half][:], in_=grouped[:]
+                )
+
+        def multiply(tt, c, lo, hi):
+            first = max(f for f, last in WEIGHT_GROUPS if f <= c)
+            n0 = (c - first) * N_TILE
+            acc = psum.tile([P, hi - lo], F32, tag="bank")
+            for g in range(PASSES):
+                half, m0 = g // 2, (g % 2) * P
+                nc.tensor.matmul_mx(
+                    out=acc[:],
+                    lhsT=codes[tt, half][:, m0 : m0 + P].bitcast(E5M2X4),
+                    lhsT_scale=scales[tt, half][:, m0 : m0 + P],
+                    rhs=words[first][:, g, 2 * (n0 + lo) : 2 * (n0 + hi)].bitcast(E2M1X4),
+                    rhs_scale=planes[first][:, g, n0 + lo : n0 + hi],
+                    start=(g == 0),
+                    stop=(g == PASSES - 1),
+                )
+            return acc
+
+        def add_bias(c, q, sums, lo, hi):
+            nc.vector.tensor_tensor(out=q[:, lo:hi], in0=sums, in1=bias[:, c * N_TILE + lo : c * N_TILE + hi], op=ADD)
+
+        def rotation_products(tt, c, q):
+            k0 = (2 - CHUNKS * c) % 3
+            heads = len(range(k0, CHUNKS, 3))
+            shape = [P, heads, ROPE // 2, 2]
+            rotated = q[:].rearrange("p (k j e) -> p k j e", j=ROPE // 2, e=2)[:, k0:CHUNKS:3, :, :]
+            pos = tt % 2
+            crossed = stage.tile(shape, F32)
+            straight = stage.tile(shape, F32)
+            nc.vector.tensor_tensor(
+                out=crossed[:], in0=rotated[:, :, :, ::-1], in1=sin_pairs[:, pos : pos + 1, :, :].broadcast_to(shape), op=MULT
+            )
+            nc.vector.tensor_tensor(
+                out=straight[:], in0=rotated, in1=cos_pairs[:, pos : pos + 1, :, :].broadcast_to(shape), op=MULT
+            )
+            return rotated, straight, crossed
+
+        def store(tt, c, q):
+            nc.sync.dma_start(out=out_rows[tt * P : (tt + 1) * P, c * N_TILE : (c + 1) * N_TILE], in_=q[:])
+
+        def rotate_and_store(tt, c, q):
+            rotated, straight, crossed = rotation_products(tt, c, q)
+            nc.gpsimd.tensor_tensor(out=rotated, in0=straight[:], in1=crossed[:], op=ADD)
+            store(tt, c, q)
+
+        nc.vector.memset(bias_rows[:].bitcast(I32), 0)
+        nc.sync.dma_start(out=bias_rows[0:BIAS_ROWS, :], in_=wq_b.rearrange("(r n) -> r n", r=BIAS_ROWS))
+        nc.scalar.dma_start(out=cos_sb[:], in_=cos.rearrange("(t p) j -> p t j", p=P))
+        nc.scalar.dma_start(out=sin_sb[:], in_=sin.rearrange("(t p) j -> p t j", p=P))
+        make_identity(nc, ident[:])
+        nc.gpsimd.tensor_copy(out=selector[:], in_=ident[:, 0:BIAS_ROWS])
+        for half in range(2):
+            nc.sync.dma_start(out=x_sb[0, half], in_=x_rows[0:P, half * HALF_K : (half + 1) * HALF_K])
+        load_x(1)
+        load_weights(*WEIGHT_GROUPS[0])
+        load_x(2)
+        load_x(3)
+        for e in range(2):
+            nc.gpsimd.tensor_copy(out=cos_pairs[:, :, :, e], in_=cos_sb[:])
+        nc.gpsimd.tensor_scalar_mul(out=sin_pairs[:, :, :, 0], in0=sin_sb[:], scalar1=-1.0)
+        nc.gpsimd.tensor_copy(out=sin_pairs[:, :, :, 1], in_=sin_sb[:])
+
+        spread_bias()
+        quantize_x(0)
+        load_weights(*WEIGHT_GROUPS[1])
+        load_weights(*WEIGHT_GROUPS[2])
+        quantize_x(1)
+        load_weights(*WEIGHT_GROUPS[3])
+
+        waiting = None
+        for c in range(COL_TILES - 1, 0, -1):
+            for tt in range(TOKEN_TILES):
+                acc = multiply(tt, c, 0, N_TILE)
+                q = results.tile([P, N_TILE], F32, tag="q")
+                add_bias(c, q, acc[:], 0, N_TILE)
+                if waiting is not None:
+                    rotate_and_store(*waiting)
+                waiting = (tt, c, q)
+                if c == COL_TILES - 1 and tt == 1:
+                    quantize_x(2)
+                    quantize_x(3)
+
+        for tt in range(TOKEN_TILES - 1):
+            acc = multiply(tt, 0, 0, N_TILE)
+            q = results.tile([P, N_TILE], F32, tag="q")
+            add_bias(0, q, acc[:, 0:384], 0, 384)
+            add_bias(0, q, acc[:, 384:512], 384, 512)
+            if tt == 0:
+                rotate_and_store(*waiting)
+            rotate_and_store(tt, 0, q)
+
+        tt = TOKEN_TILES - 1
+        q = results.tile([P, N_TILE], F32, tag="q")
+        middle = multiply(tt, 0, 128, 384)
+        left = multiply(tt, 0, 0, 128)
+        right = multiply(tt, 0, 384, 512)
+        add_bias(0, q, middle[:], 128, 384)
+        add_bias(0, q, left[:], 0, 128)
+        rotated, straight, crossed = rotation_products(tt, 0, q)
+        add_bias(0, q, right[:], 384, 512)
+        nc.vector.tensor_tensor(out=rotated, in0=straight[:], in1=crossed[:], op=ADD)
+        store(tt, 0, q)

@@ -41,22 +41,19 @@ def tile_mla_pb_kernel(tc, x, wq_w_words, wq_w_scales, wq_b, cos, sin, out):
         keep = ctx.enter_context(tc.tile_pool(name="keep", bufs=1))
         stage = ctx.enter_context(tc.tile_pool(name="stage", bufs=3))
         results = ctx.enter_context(tc.tile_pool(name="results", bufs=TOKEN_TILES * COL_TILES))
-        psum = ctx.enter_context(tc.psum_pool(name="psum", bufs=8))
+        psum = ctx.enter_context(tc.psum_pool(name="psum", bufs=7))
         ctx.enter_context(tc.manual_schedule())
 
         ident = keep.tile([P, P], F32)
-        selector = keep.tile([P, BIAS_ROWS], BF16)
+        ident_bf16 = keep.tile([P, P], BF16)
         bias_rows = keep.tile([P, BIAS_WIDTH], BF16)
         bias = keep.tile([P, COLS], BF16)
         cos_sb = keep.tile([P, 2, ROPE // 2], BF16)
         sin_sb = keep.tile([P, 2, ROPE // 2], BF16)
-        cos_pairs = keep.tile([P, 2, ROPE // 2, 2], F32)
-        sin_pairs = keep.tile([P, 2, ROPE // 2, 2], F32)
+        factors_sb = keep.tile([P, 2, 2, ROPE // 2, 2], BF16)
+        factors = psum.tile([P, 2, 2, ROPE // 2, 2], F32, bufs=1)
         x_sb, codes, scales = {}, {}, {}
-        for half in range(2):
-            first_x = keep.tile([P, HALF_K], BF16, name="x_0_%d" % half)
-            x_sb[0, half] = first_x[:]
-        for tt in range(1, TOKEN_TILES):
+        for tt in range(TOKEN_TILES):
             whole_x = keep.tile([P, DIM], BF16, name="x_%d" % tt)
             x_sb[tt] = whole_x[:]
             for half in range(2):
@@ -74,18 +71,22 @@ def tile_mla_pb_kernel(tc, x, wq_w_words, wq_w_scales, wq_b, cos, sin, out):
         def load_x(tt):
             nc.sync.dma_start(out=x_sb[tt], in_=x_rows[tt * P : (tt + 1) * P, :])
 
-        def load_weights(first, last):
+        def clear_plane(first):
+            nc.vector.memset(planes[first][:].rearrange("p g n -> p (g n)").bitcast(I32), 0)
+
+        def load_weights(first, last, pieces=1):
             plane = planes[first]
-            nc.vector.memset(plane[:].rearrange("p g n -> p (g n)").bitcast(I32), 0)
             for r in range(4):
                 nc.sync.dma_start(
                     out=plane[r:P:32, :, :].bitcast(I32),
                     in_=wq_w_scales[:, r:16:4, first * N_TILE : last * N_TILE].rearrange("g q n -> q g n").bitcast(I32),
                 )
-            nc.sync.dma_start(
-                out=words[first][:].bitcast(I32),
-                in_=wq_w_words[:, :, 2 * first * N_TILE : 2 * last * N_TILE].rearrange("g p n -> p g n").bitcast(I32),
-            )
+            step = PASSES // pieces
+            for g in range(0, PASSES, step):
+                nc.sync.dma_start(
+                    out=words[first][:, g : g + step, :].bitcast(I32),
+                    in_=wq_w_words[g : g + step, :, 2 * first * N_TILE : 2 * last * N_TILE].rearrange("g p n -> p g n").bitcast(I32),
+                )
 
         def spread_bias():
             for pair in range(BIAS_ROWS // 2):
@@ -94,12 +95,12 @@ def tile_mla_pb_kernel(tc, x, wq_w_words, wq_w_scales, wq_b, cos, sin, out):
                     row = 2 * pair + i
                     nc.tensor.matmul(
                         out=spread[:, i * BIAS_WIDTH : (i + 1) * BIAS_WIDTH],
-                        lhsT=selector[:, row : row + 1].to_broadcast([P, P]),
+                        lhsT=ident_bf16[:, row : row + 1].to_broadcast([P, P]),
                         rhs=bias_rows[:],
                         start=True,
                         stop=True,
                     )
-                nc.vector.tensor_copy(out=bias[:, 2 * pair * BIAS_WIDTH : 2 * (pair + 1) * BIAS_WIDTH], in_=spread[:])
+                nc.scalar.copy(out=bias[:, 2 * pair * BIAS_WIDTH : 2 * (pair + 1) * BIAS_WIDTH], in_=spread[:])
 
         def quantize_x(tt):
             for half in range(2):
@@ -146,10 +147,10 @@ def tile_mla_pb_kernel(tc, x, wq_w_words, wq_w_scales, wq_b, cos, sin, out):
             crossed = stage.tile(shape, F32)
             straight = stage.tile(shape, F32)
             nc.vector.tensor_tensor(
-                out=crossed[:], in0=rotated[:, :, :, ::-1], in1=sin_pairs[:, pos : pos + 1, :, :].broadcast_to(shape), op=MULT
+                out=crossed[:], in0=rotated[:, :, :, ::-1], in1=factors[:, 1, pos : pos + 1, :, :].broadcast_to(shape), op=MULT
             )
             nc.vector.tensor_tensor(
-                out=straight[:], in0=rotated, in1=cos_pairs[:, pos : pos + 1, :, :].broadcast_to(shape), op=MULT
+                out=straight[:], in0=rotated, in1=factors[:, 0, pos : pos + 1, :, :].broadcast_to(shape), op=MULT
             )
             return rotated, straight, crossed
 
@@ -161,29 +162,37 @@ def tile_mla_pb_kernel(tc, x, wq_w_words, wq_w_scales, wq_b, cos, sin, out):
             nc.gpsimd.tensor_tensor(out=rotated, in0=straight[:], in1=crossed[:], op=ADD)
             store(tt, c, q)
 
-        nc.vector.memset(bias_rows[:].bitcast(I32), 0)
+        nc.gpsimd.memset(bias_rows[:].bitcast(I32), 0)
         nc.sync.dma_start(out=bias_rows[0:BIAS_ROWS, :], in_=wq_b.rearrange("(r n) -> r n", r=BIAS_ROWS))
         nc.scalar.dma_start(out=cos_sb[:], in_=cos.rearrange("(t p) j -> p t j", p=P))
         nc.scalar.dma_start(out=sin_sb[:], in_=sin.rearrange("(t p) j -> p t j", p=P))
         make_identity(nc, ident[:])
-        nc.gpsimd.tensor_copy(out=selector[:], in_=ident[:, 0:BIAS_ROWS])
-        for half in range(2):
-            nc.sync.dma_start(out=x_sb[0, half], in_=x_rows[0:P, half * HALF_K : (half + 1) * HALF_K])
+        nc.scalar.copy(out=ident_bf16[:], in_=ident[:])
+        load_x(0)
         load_x(1)
-        load_weights(*WEIGHT_GROUPS[0])
+        clear_plane(WEIGHT_GROUPS[0][0])
+        clear_plane(WEIGHT_GROUPS[1][0])
+        load_weights(*WEIGHT_GROUPS[0], pieces=2)
         load_x(2)
         load_x(3)
+        load_weights(*WEIGHT_GROUPS[1])
         for e in range(2):
-            nc.gpsimd.tensor_copy(out=cos_pairs[:, :, :, e], in_=cos_sb[:])
-        nc.gpsimd.tensor_scalar_mul(out=sin_pairs[:, :, :, 0], in0=sin_sb[:], scalar1=-1.0)
-        nc.gpsimd.tensor_copy(out=sin_pairs[:, :, :, 1], in_=sin_sb[:])
+            nc.gpsimd.tensor_copy(out=factors_sb[:, 0, :, :, e], in_=cos_sb[:])
+        nc.gpsimd.tensor_scalar_mul(out=factors_sb[:, 1, :, :, 0], in0=sin_sb[:], scalar1=-1.0)
+        nc.gpsimd.tensor_copy(out=factors_sb[:, 1, :, :, 1], in_=sin_sb[:])
 
         spread_bias()
-        quantize_x(0)
-        load_weights(*WEIGHT_GROUPS[1])
-        load_weights(*WEIGHT_GROUPS[2])
-        quantize_x(1)
-        load_weights(*WEIGHT_GROUPS[3])
+        for tt in range(2):
+            quantize_x(tt)
+            clear_plane(WEIGHT_GROUPS[2 + tt][0])
+            load_weights(*WEIGHT_GROUPS[2 + tt])
+        nc.tensor.matmul(
+            out=factors[:].rearrange("p a t j e -> p (a t j e)"),
+            lhsT=ident_bf16[:],
+            rhs=factors_sb[:].rearrange("p a t j e -> p (a t j e)"),
+            start=True,
+            stop=True,
+        )
 
         waiting = None
         for c in range(COL_TILES - 1, 0, -1):

@@ -29,13 +29,14 @@ BIAS_ROWS = 8
 BIAS_WIDTH = COLS // BIAS_ROWS
 CHUNK = ROPE
 CHUNKS = N_TILE // CHUNK
-WEIGHT_GROUPS = [(5, 6), (4, 5), (2, 4), (0, 2)]
+WEIGHT_GROUPS = [(5, 6), (4, 5), (1, 4), (0, 1)]
+COL_ORDER = [5, 4, 2, 1, 3]
 
 
 def tile_mla_pb_kernel(tc, x, wq_w_words, wq_w_scales, wq_b, cos, sin, out):
     nc = tc.nc
-    x_rows = x.rearrange("b s k -> (b s) k")
-    out_rows = out.rearrange("b s h d -> (b s) (h d)")
+    x_rows = x.rearrange("b (p e) k -> b e p k", e=2)
+    out_rows = out.rearrange("b (p e) h d -> b e p (h d)", e=2)
 
     with ExitStack() as ctx:
         keep = ctx.enter_context(tc.tile_pool(name="keep", bufs=1))
@@ -69,10 +70,10 @@ def tile_mla_pb_kernel(tc, x, wq_w_words, wq_w_scales, wq_b, cos, sin, out):
             planes[first] = keep.tile([P, PASSES, width], U8, name="plane_%d" % first, align_bytes=64)
 
         def load_x(tt):
-            nc.sync.dma_start(out=x_sb[tt], in_=x_rows[tt * P : (tt + 1) * P, :])
+            nc.sync.dma_start(out=x_sb[tt], in_=x_rows[tt // 2, tt % 2])
 
-        def clear_plane(first):
-            nc.vector.memset(planes[first][:].rearrange("p g n -> p (g n)").bitcast(I32), 0)
+        def clear_plane(engine, first):
+            engine.memset(planes[first][:].rearrange("p g n -> p (g n)").bitcast(I32), 0)
 
         def load_weights(first, last, pieces=1):
             plane = planes[first]
@@ -100,7 +101,7 @@ def tile_mla_pb_kernel(tc, x, wq_w_words, wq_w_scales, wq_b, cos, sin, out):
                         start=True,
                         stop=True,
                     )
-                nc.scalar.copy(out=bias[:, 2 * pair * BIAS_WIDTH : 2 * (pair + 1) * BIAS_WIDTH], in_=spread[:])
+                nc.vector.tensor_copy(out=bias[:, 2 * pair * BIAS_WIDTH : 2 * (pair + 1) * BIAS_WIDTH], in_=spread[:])
 
         def quantize_x(tt):
             for half in range(2):
@@ -155,7 +156,7 @@ def tile_mla_pb_kernel(tc, x, wq_w_words, wq_w_scales, wq_b, cos, sin, out):
             return rotated, straight, crossed
 
         def store(tt, c, q):
-            nc.sync.dma_start(out=out_rows[tt * P : (tt + 1) * P, c * N_TILE : (c + 1) * N_TILE], in_=q[:])
+            nc.sync.dma_start(out=out_rows[tt // 2, tt % 2, :, c * N_TILE : (c + 1) * N_TILE], in_=q[:])
 
         def rotate_and_store(tt, c, q):
             rotated, straight, crossed = rotation_products(tt, c, q)
@@ -164,50 +165,51 @@ def tile_mla_pb_kernel(tc, x, wq_w_words, wq_w_scales, wq_b, cos, sin, out):
 
         nc.gpsimd.memset(bias_rows[:].bitcast(I32), 0)
         nc.sync.dma_start(out=bias_rows[0:BIAS_ROWS, :], in_=wq_b.rearrange("(r n) -> r n", r=BIAS_ROWS))
-        nc.scalar.dma_start(out=cos_sb[:], in_=cos.rearrange("(t p) j -> p t j", p=P))
-        nc.scalar.dma_start(out=sin_sb[:], in_=sin.rearrange("(t p) j -> p t j", p=P))
         make_identity(nc, ident[:])
         nc.scalar.copy(out=ident_bf16[:], in_=ident[:])
         load_x(0)
         load_x(1)
-        clear_plane(WEIGHT_GROUPS[0][0])
-        clear_plane(WEIGHT_GROUPS[1][0])
+        clear_plane(nc.vector, WEIGHT_GROUPS[0][0])
+        clear_plane(nc.vector, WEIGHT_GROUPS[1][0])
+        clear_plane(nc.gpsimd, WEIGHT_GROUPS[2][0])
+        clear_plane(nc.gpsimd, WEIGHT_GROUPS[3][0])
         load_weights(*WEIGHT_GROUPS[0], pieces=2)
+        nc.sync.dma_start(out=cos_sb[:], in_=cos.rearrange("(p e) j -> p e j", e=2))
+        nc.sync.dma_start(out=sin_sb[:], in_=sin.rearrange("(p e) j -> p e j", e=2))
         load_x(2)
         load_x(3)
-        load_weights(*WEIGHT_GROUPS[1])
+        for group in WEIGHT_GROUPS[1:]:
+            load_weights(*group)
         for e in range(2):
             nc.gpsimd.tensor_copy(out=factors_sb[:, 0, :, :, e], in_=cos_sb[:])
         nc.gpsimd.tensor_scalar_mul(out=factors_sb[:, 1, :, :, 0], in0=sin_sb[:], scalar1=-1.0)
         nc.gpsimd.tensor_copy(out=factors_sb[:, 1, :, :, 1], in_=sin_sb[:])
 
         spread_bias()
-        for tt in range(2):
-            quantize_x(tt)
-            clear_plane(WEIGHT_GROUPS[2 + tt][0])
-            load_weights(*WEIGHT_GROUPS[2 + tt])
-        nc.tensor.matmul(
-            out=factors[:].rearrange("p a t j e -> p (a t j e)"),
-            lhsT=ident_bf16[:],
-            rhs=factors_sb[:].rearrange("p a t j e -> p (a t j e)"),
-            start=True,
-            stop=True,
-        )
+        quantize_x(0)
+        quantize_x(1)
 
         waiting = None
-        for c in range(COL_TILES - 1, 0, -1):
+        for c in COL_ORDER:
             for tt in range(TOKEN_TILES):
                 acc = multiply(tt, c, 0, N_TILE)
                 q = results.tile([P, N_TILE], F32, tag="q")
                 add_bias(c, q, acc[:], 0, N_TILE)
-                if waiting is not None:
-                    rotate_and_store(*waiting)
-                waiting = (tt, c, q)
                 if c == COL_TILES - 1 and tt == 1:
                     quantize_x(2)
                     quantize_x(3)
+                    nc.tensor.matmul(
+                        out=factors[:].rearrange("p a t j e -> p (a t j e)"),
+                        lhsT=ident_bf16[:],
+                        rhs=factors_sb[:].rearrange("p a t j e -> p (a t j e)"),
+                        start=True,
+                        stop=True,
+                    )
+                if waiting is not None:
+                    rotate_and_store(*waiting)
+                waiting = (tt, c, q)
 
-        for tt in range(TOKEN_TILES - 1):
+        for tt in range(2):
             acc = multiply(tt, 0, 0, N_TILE)
             q = results.tile([P, N_TILE], F32, tag="q")
             add_bias(0, q, acc[:, 0:384], 0, 384)
@@ -216,14 +218,17 @@ def tile_mla_pb_kernel(tc, x, wq_w_words, wq_w_scales, wq_b, cos, sin, out):
                 rotate_and_store(*waiting)
             rotate_and_store(tt, 0, q)
 
-        tt = TOKEN_TILES - 1
-        q = results.tile([P, N_TILE], F32, tag="q")
-        middle = multiply(tt, 0, 128, 384)
-        left = multiply(tt, 0, 0, 128)
-        right = multiply(tt, 0, 384, 512)
-        add_bias(0, q, middle[:], 128, 384)
-        add_bias(0, q, left[:], 0, 128)
-        rotated, straight, crossed = rotation_products(tt, 0, q)
-        add_bias(0, q, right[:], 384, 512)
-        nc.vector.tensor_tensor(out=rotated, in0=straight[:], in1=crossed[:], op=ADD)
-        store(tt, 0, q)
+        last = {}
+        for tt in (2, 3):
+            q = results.tile([P, N_TILE], F32, tag="q")
+            last[tt] = q
+            middle = multiply(tt, 0, 128, 384)
+            add_bias(0, q, middle[:], 128, 384)
+        for tt in (2, 3):
+            rotated, straight, crossed = rotation_products(tt, 0, last[tt])
+            nc.gpsimd.tensor_tensor(out=rotated, in0=straight[:], in1=crossed[:], op=ADD)
+        for tt in (2, 3):
+            for lo in (0, 384):
+                edge = multiply(tt, 0, lo, lo + 128)
+                add_bias(0, last[tt], edge[:], lo, lo + 128)
+            store(tt, 0, last[tt])

from contextlib import ExitStack

import concourse.mybir as mybir
from concourse.masks import make_identity

B, S, DIM, H, NOPE, ROPE = 2, 256, 2048, 16, 128, 64
TOKENS = B * S
COLS = H * (NOPE + ROPE)
FLOPS = 2 * TOKENS * DIM * COLS

F32 = mybir.dt.float32
BF16 = mybir.dt.bfloat16
I32 = mybir.dt.int32
U32 = mybir.dt.uint32
U8 = mybir.dt.uint8
E5M2X4 = mybir.dt.float8_e5m2_x4
E2M1X4 = mybir.dt.float4_e2m1fn_x4
ADD = mybir.AluOpType.add
MULT = mybir.AluOpType.mult

P = 128
K_PASS = 512
PASSES = DIM // K_PASS
N_TILE = 512
TOKEN_TILES = TOKENS // P
COL_TILES = COLS // N_TILE
HALF_K = DIM // 2
BIAS_ROWS = 8
BIAS_WIDTH = COLS // BIAS_ROWS
CHUNK = ROPE
CHUNKS = N_TILE // CHUNK
WEIGHT_GROUPS = [(5, 6), (4, 5), (1, 4), (0, 1)]
COL_ORDER = [5, 4, 2, 1, 3]


def tile_mla_pb_kernel(tc, x, wq_w_words, wq_w_scales, wq_b, cos, sin, out):
    nc = tc.nc
    x_rows = x.rearrange("b (p e) k -> b e p k", e=2)
    out_rows = out.rearrange("b (p e) h d -> b e p (h d)", e=2)

    with ExitStack() as ctx:
        keep = ctx.enter_context(tc.tile_pool(name="keep", bufs=1))
        stage = ctx.enter_context(tc.tile_pool(name="stage", bufs=3))
        results = ctx.enter_context(tc.tile_pool(name="results", bufs=TOKEN_TILES * COL_TILES))
        psum = ctx.enter_context(tc.psum_pool(name="psum", bufs=7))
        ctx.enter_context(tc.manual_schedule())

        ident = keep.tile([P, P], F32)
        ident_bf16 = keep.tile([P, P], BF16)
        bias_rows = keep.tile([P, BIAS_WIDTH], BF16)
        bias = keep.tile([P, COLS], BF16)
        cos_sb = keep.tile([P, 2, ROPE // 2], BF16)
        sin_sb = keep.tile([P, 2, ROPE // 2], BF16)
        factors_sb = keep.tile([P, 2, 2, ROPE // 2, 2], BF16)
        factors = psum.tile([P, 2, 2, ROPE // 2, 2], F32, bufs=1)
        x_sb, codes, scales = {}, {}, {}
        for tt in range(TOKEN_TILES):
            whole_x = keep.tile([P, DIM], BF16, name="x_%d" % tt)
            x_sb[tt] = whole_x[:]
            for half in range(2):
                x_sb[tt, half] = whole_x[:, half * HALF_K : (half + 1) * HALF_K]
        for tt in range(TOKEN_TILES):
            for half in range(2):
                codes[tt, half] = keep.tile([P, 2 * P], U32, name="codes_%d_%d" % (tt, half), align_bytes=64)
                scales[tt, half] = keep.tile([P, 2 * P], U8, name="scales_%d_%d" % (tt, half), align_bytes=64)
        words, planes = {}, {}
        for first, last in WEIGHT_GROUPS:
            width = (last - first) * N_TILE
            words[first] = keep.tile([P, PASSES, 2 * width], U8, name="words_%d" % first, align_bytes=64)
            planes[first] = keep.tile([P, PASSES, width], U8, name="plane_%d" % first, align_bytes=64)

        def load_x(tt):
            nc.sync.dma_start(out=x_sb[tt], in_=x_rows[tt // 2, tt % 2])

        def clear_plane(engine, first):
            engine.memset(planes[first][:].rearrange("p g n -> p (g n)").bitcast(I32), 0)

        def load_weights(first, last, pieces=1):
            plane = planes[first]
            for r in range(4):
                nc.sync.dma_start(
                    out=plane[r:P:32, :, :].bitcast(I32),
                    in_=wq_w_scales[:, r:16:4, first * N_TILE : last * N_TILE].rearrange("g q n -> q g n").bitcast(I32),
                )
            step = PASSES // pieces
            for g in range(0, PASSES, step):
                nc.sync.dma_start(
                    out=words[first][:, g : g + step, :].bitcast(I32),
                    in_=wq_w_words[g : g + step, :, 2 * first * N_TILE : 2 * last * N_TILE].rearrange("g p n -> p g n").bitcast(I32),
                )

        def spread_bias():
            for pair in range(BIAS_ROWS // 2):
                spread = psum.tile([P, 2 * BIAS_WIDTH], BF16, tag="bank")
                for i in range(2):
                    row = 2 * pair + i
                    nc.tensor.matmul(
                        out=spread[:, i * BIAS_WIDTH : (i + 1) * BIAS_WIDTH],
                        lhsT=ident_bf16[:, row : row + 1].to_broadcast([P, P]),
                        rhs=bias_rows[:],
                        start=True,
                        stop=True,
                    )
                nc.vector.tensor_copy(out=bias[:, 2 * pair * BIAS_WIDTH : 2 * (pair + 1) * BIAS_WIDTH], in_=spread[:])

        def quantize_x(tt):
            for half in range(2):
                pairs = x_sb[tt, half].bitcast(F32)
                turned = psum.tile([P, 2, 2, P], F32, tag="bank")
                for g in range(2):
                    for u in range(2):
                        nc.tensor.transpose(turned[:, g, u, :], pairs[:, 256 * g + u : 256 * (g + 1) : 2], ident[:])
                grouped = stage.tile([P, HALF_K], BF16, align_bytes=64)
                nc.scalar.copy(
                    out=grouped[:].bitcast(F32).rearrange("p (g r u) -> p g r u", g=2, u=2),
                    in_=turned[:].rearrange("p g u r -> p g r u"),
                )
                nc.vector.quantize_mx(
                    out=codes[tt, half][:].bitcast(E5M2X4), scales=scales[tt, half][:], in_=grouped[:]
                )

        def multiply(tt, c, lo, hi):
            first = max(f for f, last in WEIGHT_GROUPS if f <= c)
            n0 = (c - first) * N_TILE
            acc = psum.tile([P, hi - lo], F32, tag="bank")
            for g in range(PASSES):
                half, m0 = g // 2, (g % 2) * P
                nc.tensor.matmul_mx(
                    out=acc[:],
                    lhsT=codes[tt, half][:, m0 : m0 + P].bitcast(E5M2X4),
                    lhsT_scale=scales[tt, half][:, m0 : m0 + P],
                    rhs=words[first][:, g, 2 * (n0 + lo) : 2 * (n0 + hi)].bitcast(E2M1X4),
                    rhs_scale=planes[first][:, g, n0 + lo : n0 + hi],
                    start=(g == 0),
                    stop=(g == PASSES - 1),
                )
            return acc

        def add_bias(c, q, sums, lo, hi):
            nc.vector.tensor_tensor(out=q[:, lo:hi], in0=sums, in1=bias[:, c * N_TILE + lo : c * N_TILE + hi], op=ADD)

        def rotation_products(tt, c, q):
            k0 = (2 - CHUNKS * c) % 3
            heads = len(range(k0, CHUNKS, 3))
            shape = [P, heads, ROPE // 2, 2]
            rotated = q[:].rearrange("p (k j e) -> p k j e", j=ROPE // 2, e=2)[:, k0:CHUNKS:3, :, :]
            pos = tt % 2
            crossed = stage.tile(shape, F32)
            straight = stage.tile(shape, F32)
            nc.vector.tensor_tensor(
                out=crossed[:], in0=rotated[:, :, :, ::-1], in1=factors[:, 1, pos : pos + 1, :, :].broadcast_to(shape), op=MULT
            )
            nc.vector.tensor_tensor(
                out=straight[:], in0=rotated, in1=factors[:, 0, pos : pos + 1, :, :].broadcast_to(shape), op=MULT
            )
            return rotated, straight, crossed

        def store(tt, c, q):
            nc.sync.dma_start(out=out_rows[tt // 2, tt % 2, :, c * N_TILE : (c + 1) * N_TILE], in_=q[:])

        def rotate_and_store(tt, c, q):
            rotated, straight, crossed = rotation_products(tt, c, q)
            nc.gpsimd.tensor_tensor(out=rotated, in0=straight[:], in1=crossed[:], op=ADD)
            store(tt, c, q)

        nc.gpsimd.memset(bias_rows[:].bitcast(I32), 0)
        nc.sync.dma_start(out=bias_rows[0:BIAS_ROWS, :], in_=wq_b.rearrange("(r n) -> r n", r=BIAS_ROWS))
        make_identity(nc, ident[:])
        nc.scalar.copy(out=ident_bf16[:], in_=ident[:])
        load_x(0)
        load_x(1)
        clear_plane(nc.vector, WEIGHT_GROUPS[0][0])
        clear_plane(nc.vector, WEIGHT_GROUPS[1][0])
        clear_plane(nc.gpsimd, WEIGHT_GROUPS[2][0])
        clear_plane(nc.gpsimd, WEIGHT_GROUPS[3][0])
        load_weights(*WEIGHT_GROUPS[0], pieces=2)
        nc.sync.dma_start(out=cos_sb[:], in_=cos.rearrange("(p e) j -> p e j", e=2))
        nc.sync.dma_start(out=sin_sb[:], in_=sin.rearrange("(p e) j -> p e j", e=2))
        load_x(2)
        load_x(3)
        for group in WEIGHT_GROUPS[1:]:
            load_weights(*group)
        for e in range(2):
            nc.gpsimd.tensor_copy(out=factors_sb[:, 0, :, :, e], in_=cos_sb[:])
        nc.gpsimd.tensor_scalar_mul(out=factors_sb[:, 1, :, :, 0], in0=sin_sb[:], scalar1=-1.0)
        nc.gpsimd.tensor_copy(out=factors_sb[:, 1, :, :, 1], in_=sin_sb[:])

        spread_bias()
        quantize_x(0)
        quantize_x(1)

        waiting = None
        for c in COL_ORDER:
            for tt in range(TOKEN_TILES):
                acc = multiply(tt, c, 0, N_TILE)
                q = results.tile([P, N_TILE], F32, tag="q")
                add_bias(c, q, acc[:], 0, N_TILE)
                if c == COL_TILES - 1 and tt == 1:
                    quantize_x(2)
                    quantize_x(3)
                    nc.tensor.matmul(
                        out=factors[:].rearrange("p a t j e -> p (a t j e)"),
                        lhsT=ident_bf16[:],
                        rhs=factors_sb[:].rearrange("p a t j e -> p (a t j e)"),
                        start=True,
                        stop=True,
                    )
                if waiting is not None:
                    rotate_and_store(*waiting)
                waiting = (tt, c, q)

        for tt in range(2):
            acc = multiply(tt, 0, 0, N_TILE)
            q = results.tile([P, N_TILE], F32, tag="q")
            add_bias(0, q, acc[:, 0:384], 0, 384)
            add_bias(0, q, acc[:, 384:512], 384, 512)
            if tt == 0:
                rotate_and_store(*waiting)
            rotate_and_store(tt, 0, q)

        last = {}
        for tt in (2, 3):
            q = results.tile([P, N_TILE], F32, tag="q")
            last[tt] = q
            middle = multiply(tt, 0, 128, 384)
            add_bias(0, q, middle[:], 128, 384)
        for tt in (2, 3):
            rotated, straight, crossed = rotation_products(tt, 0, last[tt])
            nc.gpsimd.tensor_tensor(out=rotated, in0=straight[:], in1=crossed[:], op=ADD)
        for tt in (2, 3):
            for lo in (0, 384):
                edge = multiply(tt, 0, lo, lo + 128)
                add_bias(0, last[tt], edge[:], lo, lo + 128)
            store(tt, 0, last[tt])
